import numpy as np
import ml_dtypes


def mxq(x, axis, fmt="e4m3"):
    dtype, down = {"e4m3": (ml_dtypes.float8_e4m3fn, 7), "e5m2": (ml_dtypes.float8_e5m2, 14)}[fmt]
    v = np.moveaxis(np.asarray(x, np.float32).astype(ml_dtypes.bfloat16).astype(np.float64), axis, -1)
    blocks = v.reshape(v.shape[:-1] + (-1, 32))
    amax = np.abs(blocks).max(-1, keepdims=True)
    byte = np.maximum(np.where(amax > 0, np.frexp(amax)[1] - 1 + 127, 0) - down, 1)
    scale = np.exp2(byte - 127.0)
    codes = (blocks / scale).astype(np.float32).astype(dtype).astype(np.float64)
    return np.moveaxis((codes * scale).reshape(v.shape), -1, axis)


WIDE = False


def mx_kscale(k):
    if not WIDE:
        return np.ones(k)
    levels = np.array([10, -10, 5, -5, 0])
    a = np.random.permutation(np.resize(levels, k // 512 * 4)).reshape(k // 512, 4)
    idx = np.arange(k)
    return np.exp2(a[idx // 512, idx % 128 // 32])


BF16 = ml_dtypes.bfloat16


def bf(x):
    return np.asarray(x, np.float32).astype(BF16)


def f64(x):
    return np.asarray(x).astype(np.float64)


E2M1 = np.array([0.0, 0.5, 1.0, 1.5, 2.0, 3.0, 4.0, 6.0, -0.0, -0.5, -1.0, -1.5, -2.0, -3.0, -4.0, -6.0])


def pack_weight(w, fmt):
    k, n = w.shape
    w = f64(bf(w)).reshape(k // 32, 32, n)
    amax = np.abs(w).max(1)
    if fmt == "e4m3":
        byte = np.frexp(amax)[1] - 1 + 127 - 7
    else:
        mant, ex = np.frexp(amax / 6.0)
        byte = np.where(mant > 0.5, ex, ex - 1) + 127
    byte = np.clip(np.where(amax > 0, byte, 1), 1, 254)
    scaled = (w * np.exp2(127.0 - byte)[:, None, :]).reshape(k, n).astype(np.float32)
    by_word = np.ascontiguousarray(scaled.reshape(k // 512, 128, 4, n).transpose(0, 1, 3, 2))
    if fmt == "e4m3":
        words = by_word.astype(ml_dtypes.float8_e4m3fn).view(np.uint8)
    else:
        c = by_word.astype(ml_dtypes.float4_e2m1fn).view(np.uint8) & 0xF
        words = c[..., 0::2] | (c[..., 1::2] << 4)
    return np.ascontiguousarray(words), np.ascontiguousarray(byte.astype(np.uint8).reshape(k // 512, 16, n))


def unpack_weight(words, scales, fmt):
    g, p, n, _ = words.shape
    if fmt == "e4m3":
        vals = np.ascontiguousarray(words).view(ml_dtypes.float8_e4m3fn).astype(np.float64)
    else:
        nib = np.empty((g, p, n, 4), np.uint8)
        nib[..., 0::2] = words & 0xF
        nib[..., 1::2] = words >> 4
        vals = E2M1[nib]
    vals = vals * np.repeat(np.exp2(scales.astype(np.float64) - 127.0), 8, axis=1)[..., None]
    return vals.transpose(0, 1, 3, 2).reshape(g * 512, n)

def pack4(w):
    words, scales = pack_weight(w, "e2m1")
    return words.reshape(words.shape[0], 128, -1), scales


def unpack4(words, scales):
    return unpack_weight(words.reshape(words.shape[0], 128, -1, 2), scales, "e2m1")


B, G, DB, DR = 128, 16, 1024, 2048


def mish(v):
    return v * np.tanh(np.log(1.0 + np.exp(v)))


def setup_inputs():
    s, t = mx_kscale(DR), mx_kscale(DB)
    BB_feature = bf(np.random.standard_normal((B, G, DB)) * t)
    RF_feature = bf(np.random.standard_normal((B, DR)) * s)
    W_bbbb = np.random.standard_normal((DB, DB)) / np.sqrt(DB) / t
    b_bbbb = bf(np.random.standard_normal(DB) * 0.5)
    W_rfbb = np.random.standard_normal((DB, DR)) / np.sqrt(DR) / s
    b_rfbb = bf(np.random.standard_normal(DB) * 0.5)
    W_bbbb_words, W_bbbb_scales = pack4(np.ascontiguousarray(W_bbbb.T))
    W_rfbb_words, W_rfbb_scales = pack4(np.ascontiguousarray(W_rfbb.T))
    return {"BB_feature": BB_feature,
            "RF_feature": RF_feature,
            "W_bbbb_words": W_bbbb_words,
            "W_bbbb_scales": W_bbbb_scales,
            "b_bbbb": b_bbbb,
            "W_rfbb_words": W_rfbb_words,
            "W_rfbb_scales": W_rfbb_scales,
            "b_rfbb": b_rfbb}


def reference(BB_feature, RF_feature, W_bbbb_words, W_bbbb_scales, b_bbbb, W_rfbb_words, W_rfbb_scales, b_rfbb):
    RF_to_BB = mish((mxq(f64(RF_feature), 1, "e4m3") @ unpack4(W_rfbb_words, W_rfbb_scales)) + f64(b_rfbb))
    BB_to_BB = mish((mxq(f64(BB_feature), 2, "e4m3") @ unpack4(W_bbbb_words, W_bbbb_scales)) + f64(b_bbbb))
    return BB_to_BB + RF_to_BB[:, None, :]

@@ -1,0 +1,193 @@
+import concourse.mybir as mybir
+from concourse.masks import make_identity
+
+F32 = mybir.dt.float32
+BF16 = mybir.dt.bfloat16
+I32 = mybir.dt.int32
+U32 = mybir.dt.uint32
+U8 = mybir.dt.uint8
+FP8X4 = mybir.dt.float8_e4m3fn_x4
+FP4X4 = mybir.dt.float4_e2m1fn_x4
+ACT = mybir.ActivationFunctionType
+ALU = mybir.AluOpType
+
+P = 128
+GROUPS = 16
+DB = 1024
+DR = 2048
+K_PASS = 512
+UNIT = 2 * K_PASS
+N_HALF = 512
+HALVES = DB // N_HALF
+BATCH = 4
+LN_FLOOR = 2.0**-60
+
+FLOPS = 2 * (P * GROUPS * DB * DB + P * DR * DB)
+
+
+def tile_gnn_layer_pb_kernel(
+    tc, BB_feature, RF_feature, W_bbbb_words, W_bbbb_scales, b_bbbb, W_rfbb_words, W_rfbb_scales, b_rfbb, out
+):
+    nc = tc.nc
+    with (
+        tc.tile_pool(name="keep", bufs=1) as keep,
+        tc.tile_pool(name="work", bufs=4) as work,
+        tc.psum_pool(name="flipped", bufs=2) as flipped,
+        tc.psum_pool(name="sums", bufs=4) as sums,
+        tc.manual_schedule(),
+    ):
+        x_bb = keep.tile([P, GROUPS, DB], BF16)
+        x_rf = keep.tile([P, DR], BF16)
+        w_bb = keep.tile([P, DB // K_PASS, 2 * DB], U8, align_bytes=64)
+        w_rf = keep.tile([P, DR // K_PASS, 2 * DB], U8, align_bytes=64)
+        w_bb_scales = keep.tile([P, DB // K_PASS, DB], U8, align_bytes=64)
+        w_rf_scales = keep.tile([P, DR // K_PASS, DB], U8, align_bytes=64)
+        identity = keep.tile([P, P], F32)
+        ones = keep.tile([P, P], BF16)
+        bias_rows = keep.tile([P, 2 * DB], BF16)
+        bias = keep.tile([P, 2 * DB], F32)
+        ln_floor = keep.tile([P, 1], F32)
+        v_bb = keep.tile([P, GROUPS, DB], F32)
+        m_bb = keep.tile([P, GROUPS, DB], F32)
+        v_rf = keep.tile([P, DB], F32)
+        m_rf = keep.tile([P, DB], F32)
+
+        nc.vector.memset(w_bb_scales[:].bitcast(I32), 0)
+        nc.vector.memset(w_rf_scales[:].bitcast(I32), 0)
+        nc.vector.memset(ln_floor[:], LN_FLOOR)
+        nc.gpsimd.memset(bias_rows[:], 0.0)
+        nc.gpsimd.memset(ones[:], 1.0)
+        make_identity(nc, identity[:])
+
+        def load_scales(planes, scales):
+            for r in range(4):
+                nc.sync.dma_start(
+                    out=planes[r:P:32, :, :].bitcast(I32),
+                    in_=scales.bitcast(I32)[:, r:16:4, :].rearrange("c q n -> q c n"),
+                )
+
+        def load_words(words_tile, words):
+            nc.sync.dma_start(out=words_tile[:].bitcast(I32), in_=words.bitcast(I32).rearrange("c p n -> p c n"))
+
+        nc.scalar.dma_start(out=bias_rows[0:1, 0:DB], in_=b_bbbb.unsqueeze(0))
+        nc.scalar.dma_start(out=bias_rows[0:1, DB : 2 * DB], in_=b_rfbb.unsqueeze(0))
+        nc.sync.dma_start(out=x_bb[:, 0, :], in_=BB_feature[:, 0, :])
+        load_scales(w_bb_scales, W_bbbb_scales)
+        load_words(w_bb, W_bbbb_words)
+        for g in range(1, BATCH):
+            nc.sync.dma_start(out=x_bb[:, g, :], in_=BB_feature[:, g, :])
+        nc.sync.dma_start(out=x_rf[:], in_=RF_feature)
+        load_scales(w_rf_scales, W_rfbb_scales)
+        load_words(w_rf, W_rfbb_words)
+        for g in range(BATCH, GROUPS):
+            nc.sync.dma_start(out=x_bb[:, g, :], in_=BB_feature[:, g, :])
+
+        for j in range(2 * HALVES):
+            cols = slice(j * N_HALF, (j + 1) * N_HALF)
+            spread = sums.tile([P, N_HALF], F32, tag="acc")
+            nc.tensor.matmul(out=spread[:], lhsT=ones[:], rhs=bias_rows[:, cols], start=True, stop=True)
+            nc.scalar.copy(out=bias[:, cols], in_=spread[:])
+
+        bb_rows = [
+            {
+                "x": x_bb[:, g, :],
+                "w": w_bb,
+                "w_scales": w_bb_scales,
+                "bias": bias[:, 0:DB],
+                "v": v_bb[:, g, :],
+                "m": m_bb[:, g, :],
+            }
+            for g in range(GROUPS)
+        ]
+        rf_row = {
+            "x": x_rf[:],
+            "w": w_rf,
+            "w_scales": w_rf_scales,
+            "bias": bias[:, DB : 2 * DB],
+            "v": v_rf[:],
+            "m": m_rf[:],
+        }
+        rows = bb_rows[:BATCH] + [rf_row] + bb_rows[BATCH:]
+
+        def transpose_and_regroup(row):
+            words = row["x"].bitcast(F32)
+            grouped_units = []
+            for unit in range(words.shape[1] * 2 // UNIT):
+                xt = flipped.tile([P, 2, 2, P], F32)
+                for c in range(2):
+                    for u in range(2):
+                        first = (2 * unit + c) * (K_PASS // 2)
+                        nc.tensor.transpose(xt[:, c, u, :], words[:, first + u : first + K_PASS // 2 : 2], identity[:])
+                grouped = work.tile([P, UNIT], BF16, align_bytes=64)
+                nc.vector.tensor_copy(
+                    out=grouped[:].bitcast(F32).rearrange("p (c r u) -> p c r u", c=2, u=2),
+                    in_=xt[:].rearrange("p c u r -> p c r u"),
+                )
+                grouped_units.append(grouped)
+            return grouped_units
+
+        def quantise(grouped_units):
+            quantised_units = []
+            for grouped in grouped_units:
+                codes = work.tile([P, 2 * P], U32, align_bytes=64)
+                scales = work.tile([P, 2 * P], U8, align_bytes=64)
+                nc.vector.quantize_mx(out=codes[:].bitcast(FP8X4), scales=scales[:], in_=grouped[:])
+                quantised_units.append((codes, scales))
+            return quantised_units
+
+        def multiply(row, quantised_units):
+            passes = 2 * len(quantised_units)
+            accs = []
+            for h in range(HALVES):
+                acc = sums.tile([P, N_HALF], F32)
+                for c in range(passes):
+                    codes, scales = quantised_units[c // 2]
+                    x_cols = slice((c % 2) * P, (c % 2 + 1) * P)
+                    nc.tensor.matmul_mx(
+                        out=acc[:],
+                        lhsT=codes[:, x_cols].bitcast(FP8X4),
+                        lhsT_scale=scales[:, x_cols],
+                        rhs=row["w"][:, c, 2 * h * N_HALF : 2 * (h + 1) * N_HALF].bitcast(FP4X4),
+                        rhs_scale=row["w_scales"][:, c, h * N_HALF : (h + 1) * N_HALF],
+                        start=(c == 0),
+                        stop=(c == passes - 1),
+                    )
+                accs.append(acc)
+            return accs
+
+        def add_bias(row, accs):
+            for h in range(HALVES):
+                cols = slice(h * N_HALF, (h + 1) * N_HALF)
+                nc.vector.tensor_tensor(out=row["v"][:, cols], in0=accs[h][:], in1=row["bias"][:, cols], op=ALU.add)
+
+        grouped_of = {}
+        accs_of = {}
+        for step in range(len(rows) + 2):
+            if step < len(rows):
+                grouped_of[step] = transpose_and_regroup(rows[step])
+            if 1 <= step <= len(rows):
+                accs_of[step - 1] = multiply(rows[step - 1], quantise(grouped_of[step - 1]))
+            if step >= 2:
+                add_bias(rows[step - 2], accs_of[step - 2])
+
+        batches = [rows[: BATCH + 1]] + [rows[b * BATCH + 1 : (b + 1) * BATCH + 1] for b in range(1, GROUPS // BATCH)]
+
+        def sigmoid(batch):
+            for row in batch:
+                nc.scalar.activation(out=row["m"], in_=row["v"], func=ACT.Sigmoid, scale=-1.0)
+
+        sigmoid(batches[0])
+        group = 0
+        for b in range(len(batches)):
+            for row in batches[b]:
+                nc.scalar.activation(out=row["m"], in_=row["m"], func=ACT.Ln, bias=ln_floor[:])
+            if b + 1 < len(batches):
+                sigmoid(batches[b + 1])
+            for row in batches[b]:
+                nc.scalar.activation(out=row["m"], in_=row["m"], func=ACT.Tanh, scale=-1.0)
+                nc.gpsimd.tensor_tensor(out=row["m"], in0=row["m"], in1=row["v"], op=ALU.mult)
+            for row in batches[b]:
+                if row is not rf_row:
+                    nc.vector.tensor_tensor(out=row["m"], in0=row["m"], in1=m_rf[:], op=ALU.add)
+                    nc.sync.dma_start(out=out[:, group, :], in_=row["m"])
+                    group += 1

@@ -32,7 +32,7 @@ def tile_gnn_layer_pb_kernel(
     with (
         tc.tile_pool(name="keep", bufs=1) as keep,
         tc.tile_pool(name="work", bufs=4) as work,
-        tc.psum_pool(name="flipped", bufs=2) as flipped,
+        tc.psum_pool(name="flipped", bufs=3) as flipped,
         tc.psum_pool(name="sums", bufs=4) as sums,
         tc.manual_schedule(),
     ):
@@ -160,15 +160,19 @@ def tile_gnn_layer_pb_kernel(
                 cols = slice(h * N_HALF, (h + 1) * N_HALF)
                 nc.vector.tensor_tensor(out=row["v"][:, cols], in0=accs[h][:], in1=row["bias"][:, cols], op=ALU.add)
 
+        last = len(rows) - 1
         grouped_of = {}
+        quantised_of = {}
         accs_of = {}
-        for step in range(len(rows) + 2):
-            if step < len(rows):
+        for step in range(len(rows) + 3):
+            if step <= last:
                 grouped_of[step] = transpose_and_regroup(rows[step])
-            if 1 <= step <= len(rows):
-                accs_of[step - 1] = multiply(rows[step - 1], quantise(grouped_of[step - 1]))
-            if step >= 2:
-                add_bias(rows[step - 2], accs_of[step - 2])
+            if 0 <= step - 1 <= last:
+                quantised_of[step - 1] = quantise(grouped_of[step - 1])
+            if 0 <= step - 2 <= last:
+                accs_of[step - 2] = multiply(rows[step - 2], quantised_of[step - 2])
+            if 0 <= step - 3:
+                add_bias(rows[step - 3], accs_of[step - 3])
 
         batches = [rows[: BATCH + 1]] + [rows[b * BATCH + 1 : (b + 1) * BATCH + 1] for b in range(1, GROUPS // BATCH)]
 

@@ -19,7 +19,8 @@ K_PASS = 512
 UNIT = 2 * K_PASS
 N_HALF = 512
 HALVES = DB // N_HALF
-BATCH = 4
+BATCH = 5
+FIRST_BATCH = 3
 LN_FLOOR = 2.0**-60
 
 FLOPS = 2 * (P * GROUPS * DB * DB + P * DR * DB)
@@ -74,12 +75,12 @@ def tile_gnn_layer_pb_kernel(
         nc.sync.dma_start(out=x_bb[:, 0, :], in_=BB_feature[:, 0, :])
         load_scales(w_bb_scales, W_bbbb_scales)
         load_words(w_bb, W_bbbb_words)
-        for g in range(1, BATCH):
+        for g in range(1, FIRST_BATCH):
             nc.sync.dma_start(out=x_bb[:, g, :], in_=BB_feature[:, g, :])
         nc.sync.dma_start(out=x_rf[:], in_=RF_feature)
         load_scales(w_rf_scales, W_rfbb_scales)
         load_words(w_rf, W_rfbb_words)
-        for g in range(BATCH, GROUPS):
+        for g in range(FIRST_BATCH, GROUPS):
             nc.sync.dma_start(out=x_bb[:, g, :], in_=BB_feature[:, g, :])
 
         for j in range(2 * HALVES):
@@ -96,6 +97,7 @@ def tile_gnn_layer_pb_kernel(
                 "bias": bias[:, 0:DB],
                 "v": v_bb[:, g, :],
                 "m": m_bb[:, g, :],
+                "out": out[:, g, :],
             }
             for g in range(GROUPS)
         ]
@@ -107,17 +109,24 @@ def tile_gnn_layer_pb_kernel(
             "v": v_rf[:],
             "m": m_rf[:],
         }
-        rows = bb_rows[:BATCH] + [rf_row] + bb_rows[BATCH:]
+        bb_batches = [bb_rows[:FIRST_BATCH]] + [bb_rows[first : first + BATCH] for first in range(FIRST_BATCH, GROUPS, BATCH)]
+        rows = bb_batches[0] + [rf_row] + bb_rows[FIRST_BATCH:]
 
-        def transpose_and_regroup(row):
+        def transpose(row):
             words = row["x"].bitcast(F32)
-            grouped_units = []
+            flipped_units = []
             for unit in range(words.shape[1] * 2 // UNIT):
                 xt = flipped.tile([P, 2, 2, P], F32)
                 for c in range(2):
                     for u in range(2):
                         first = (2 * unit + c) * (K_PASS // 2)
                         nc.tensor.transpose(xt[:, c, u, :], words[:, first + u : first + K_PASS // 2 : 2], identity[:])
+                flipped_units.append(xt)
+            return flipped_units
+
+        def regroup(flipped_units):
+            grouped_units = []
+            for xt in flipped_units:
                 grouped = work.tile([P, UNIT], BF16, align_bytes=64)
                 nc.vector.tensor_copy(
                     out=grouped[:].bitcast(F32).rearrange("p (c r u) -> p c r u", c=2, u=2),
@@ -160,38 +169,36 @@ def tile_gnn_layer_pb_kernel(
                 cols = slice(h * N_HALF, (h + 1) * N_HALF)
                 nc.vector.tensor_tensor(out=row["v"][:, cols], in0=accs[h][:], in1=row["bias"][:, cols], op=ALU.add)
 
-        last = len(rows) - 1
+        flipped_of = {}
         grouped_of = {}
-        quantised_of = {}
         accs_of = {}
-        for step in range(len(rows) + 3):
-            if step <= last:
-                grouped_of[step] = transpose_and_regroup(rows[step])
-            if 0 <= step - 1 <= last:
-                quantised_of[step - 1] = quantise(grouped_of[step - 1])
-            if 0 <= step - 2 <= last:
-                accs_of[step - 2] = multiply(rows[step - 2], quantised_of[step - 2])
-            if 0 <= step - 3:
-                add_bias(rows[step - 3], accs_of[step - 3])
-
-        batches = [rows[: BATCH + 1]] + [rows[b * BATCH + 1 : (b + 1) * BATCH + 1] for b in range(1, GROUPS // BATCH)]
+        for i in range(-2, len(rows) + 1):
+            if 0 <= i < len(rows):
+                accs_of[i] = multiply(rows[i], quantise(grouped_of[i]))
+            if i + 2 < len(rows):
+                flipped_of[i + 2] = transpose(rows[i + 2])
+            if 0 <= i + 1 < len(rows):
+                grouped_of[i + 1] = regroup(flipped_of[i + 1])
+            if 0 <= i - 1:
+                add_bias(rows[i - 1], accs_of[i - 1])
 
         def sigmoid(batch):
             for row in batch:
                 nc.scalar.activation(out=row["m"], in_=row["v"], func=ACT.Sigmoid, scale=-1.0)
 
-        sigmoid(batches[0])
-        group = 0
-        for b in range(len(batches)):
-            for row in batches[b]:
+        sigmoid(bb_batches[0] + [rf_row])
+        for b in range(len(bb_batches)):
+            batch = ([rf_row] if b == 0 else []) + bb_batches[b]
+            for row in batch:
                 nc.scalar.activation(out=row["m"], in_=row["m"], func=ACT.Ln, bias=ln_floor[:])
-            if b + 1 < len(batches):
-                sigmoid(batches[b + 1])
-            for row in batches[b]:
+            if b + 1 < len(bb_batches):
+                sigmoid(bb_batches[b + 1])
+            for row in batch:
                 nc.scalar.activation(out=row["m"], in_=row["m"], func=ACT.Tanh, scale=-1.0)
-                nc.gpsimd.tensor_tensor(out=row["m"], in0=row["m"], in1=row["v"], op=ALU.mult)
-            for row in batches[b]:
+                halves = [slice(h * N_HALF, (h + 1) * N_HALF) for h in range(HALVES)]
+                for cols in halves:
+                    nc.vector.tensor_tensor(out=row["m"][:, cols], in0=row["m"][:, cols], in1=row["v"][:, cols], op=ALU.mult)
                 if row is not rf_row:
-                    nc.vector.tensor_tensor(out=row["m"], in0=row["m"], in1=m_rf[:], op=ALU.add)
-                    nc.sync.dma_start(out=out[:, group, :], in_=row["m"])
-                    group += 1
+                    for cols in halves:
+                        nc.vector.tensor_tensor(out=row["m"][:, cols], in0=row["m"][:, cols], in1=m_rf[:, cols], op=ALU.add)
+                    nc.sync.dma_start(out=row["out"], in_=row["m"])

@@ -54,11 +54,11 @@ def tile_gnn_layer_pb_kernel(
         m_rf = keep.tile([P, DB], F32)
 
         nc.vector.memset(w_bb_scales[:].bitcast(I32), 0)
+        nc.vector.memset(bias_rows[:].bitcast(I32), 0)
         nc.vector.memset(w_rf_scales[:].bitcast(I32), 0)
         nc.vector.memset(ln_floor[:], LN_FLOOR)
-        nc.gpsimd.memset(bias_rows[:], 0.0)
-        nc.gpsimd.memset(ones[:], 1.0)
         make_identity(nc, identity[:])
+        nc.gpsimd.memset(ones[:], 1.0)
 
         def load_scales(planes, scales):
             for r in range(4):
@@ -72,22 +72,17 @@ def tile_gnn_layer_pb_kernel(
 
         nc.scalar.dma_start(out=bias_rows[0:1, 0:DB], in_=b_bbbb.unsqueeze(0))
         nc.scalar.dma_start(out=bias_rows[0:1, DB : 2 * DB], in_=b_rfbb.unsqueeze(0))
-        nc.sync.dma_start(out=x_bb[:, 0, :], in_=BB_feature[:, 0, :])
+        for g in range(2):
+            nc.sync.dma_start(out=x_bb[:, g, :], in_=BB_feature[:, g, :])
         load_scales(w_bb_scales, W_bbbb_scales)
         load_words(w_bb, W_bbbb_words)
-        for g in range(1, FIRST_BATCH):
+        for g in range(2, FIRST_BATCH):
             nc.sync.dma_start(out=x_bb[:, g, :], in_=BB_feature[:, g, :])
         nc.sync.dma_start(out=x_rf[:], in_=RF_feature)
         load_scales(w_rf_scales, W_rfbb_scales)
         load_words(w_rf, W_rfbb_words)
         for g in range(FIRST_BATCH, GROUPS):
             nc.sync.dma_start(out=x_bb[:, g, :], in_=BB_feature[:, g, :])
-
-        for j in range(2 * HALVES):
-            cols = slice(j * N_HALF, (j + 1) * N_HALF)
-            spread = sums.tile([P, N_HALF], F32, tag="acc")
-            nc.tensor.matmul(out=spread[:], lhsT=ones[:], rhs=bias_rows[:, cols], start=True, stop=True)
-            nc.scalar.copy(out=bias[:, cols], in_=spread[:])
 
         bb_rows = [
             {
@@ -164,41 +159,56 @@ def tile_gnn_layer_pb_kernel(
                 accs.append(acc)
             return accs
 
-        def add_bias(row, accs):
-            for h in range(HALVES):
-                cols = slice(h * N_HALF, (h + 1) * N_HALF)
-                nc.vector.tensor_tensor(out=row["v"][:, cols], in0=accs[h][:], in1=row["bias"][:, cols], op=ALU.add)
+        def add_bias(row, accs, h):
+            cols = slice(h * N_HALF, (h + 1) * N_HALF)
+            nc.vector.tensor_tensor(out=row["v"][:, cols], in0=accs[h][:], in1=row["bias"][:, cols], op=ALU.add)
 
-        flipped_of = {}
-        grouped_of = {}
+        flipped_of = {0: transpose(rows[0]), 1: transpose(rows[1])}
+        grouped_of = {0: regroup(flipped_of[0])}
         accs_of = {}
-        for i in range(-2, len(rows) + 1):
-            if 0 <= i < len(rows):
+
+        for j in range(2 * HALVES):
+            cols = slice(j * N_HALF, (j + 1) * N_HALF)
+            spread = sums.tile([P, N_HALF], F32, tag="acc")
+            nc.tensor.matmul(out=spread[:], lhsT=ones[:], rhs=bias_rows[:, cols], start=True, stop=True)
+            nc.scalar.copy(out=bias[:, cols], in_=spread[:])
+
+        for i in range(len(rows) + 1):
+            if i < len(rows):
                 accs_of[i] = multiply(rows[i], quantise(grouped_of[i]))
             if i + 2 < len(rows):
                 flipped_of[i + 2] = transpose(rows[i + 2])
-            if 0 <= i + 1 < len(rows):
+            if i >= 1:
+                add_bias(rows[i - 1], accs_of[i - 1], 0)
+            if i + 1 < len(rows):
                 grouped_of[i + 1] = regroup(flipped_of[i + 1])
-            if 0 <= i - 1:
-                add_bias(rows[i - 1], accs_of[i - 1])
+            if i >= 1:
+                add_bias(rows[i - 1], accs_of[i - 1], 1)
 
         def sigmoid(batch):
             for row in batch:
                 nc.scalar.activation(out=row["m"], in_=row["v"], func=ACT.Sigmoid, scale=-1.0)
 
-        sigmoid(bb_batches[0] + [rf_row])
-        for b in range(len(bb_batches)):
-            batch = ([rf_row] if b == 0 else []) + bb_batches[b]
-            for row in batch:
+        batches = [bb_batches[0], [rf_row] + bb_batches[1]] + bb_batches[2:]
+        halves = [slice(h * N_HALF, (h + 1) * N_HALF) for h in range(HALVES)]
+        sigmoid(batches[0])
+        lacking_rf = []
+        for b in range(len(batches)):
+            for row in batches[b]:
                 nc.scalar.activation(out=row["m"], in_=row["m"], func=ACT.Ln, bias=ln_floor[:])
-            if b + 1 < len(bb_batches):
-                sigmoid(bb_batches[b + 1])
-            for row in batch:
+            if b + 1 < len(batches):
+                sigmoid(batches[b + 1])
+            for row in batches[b]:
                 nc.scalar.activation(out=row["m"], in_=row["m"], func=ACT.Tanh, scale=-1.0)
-                halves = [slice(h * N_HALF, (h + 1) * N_HALF) for h in range(HALVES)]
                 for cols in halves:
                     nc.vector.tensor_tensor(out=row["m"][:, cols], in0=row["m"][:, cols], in1=row["v"][:, cols], op=ALU.mult)
                 if row is not rf_row:
-                    for cols in halves:
-                        nc.vector.tensor_tensor(out=row["m"][:, cols], in0=row["m"][:, cols], in1=m_rf[:, cols], op=ALU.add)
-                    nc.sync.dma_start(out=row["out"], in_=row["m"])
+                    lacking_rf.append(row)
+                if b >= 1:
+                    for late in lacking_rf:
+                        for cols in halves:
+                            nc.vector.tensor_tensor(
+                                out=late["m"][:, cols], in0=late["m"][:, cols], in1=m_rf[:, cols], op=ALU.add
+                            )
+                            nc.sync.dma_start(out=late["out"][:, cols], in_=late["m"][:, cols])
+                    lacking_rf = []

@@ -19,8 +19,10 @@ K_PASS = 512
 UNIT = 2 * K_PASS
 N_HALF = 512
 HALVES = DB // N_HALF
-BATCH = 5
 FIRST_BATCH = 3
+PER = 1
+S_ROWS = (1, 2, 3, 4)
+BATCHES = ((0, 1, 2), ("rf", 3, 4, 5, 6, 7, 8, 9, 10), (11, 12, 13, 14), (15,))
 LN_FLOOR = 2.0**-60
 
 FLOPS = 2 * (P * GROUPS * DB * DB + P * DR * DB)
@@ -48,6 +50,7 @@ def tile_gnn_layer_pb_kernel(
         bias_rows = keep.tile([P, 2 * DB], BF16)
         bias = keep.tile([P, 2 * DB], F32)
         ln_floor = keep.tile([P, 1], F32)
+        warm = keep.tile([P, 1], F32)
         v_bb = keep.tile([P, GROUPS, DB], F32)
         m_bb = keep.tile([P, GROUPS, DB], F32)
         v_rf = keep.tile([P, DB], F32)
@@ -74,8 +77,8 @@ def tile_gnn_layer_pb_kernel(
         nc.scalar.dma_start(out=bias_rows[0:1, DB : 2 * DB], in_=b_rfbb.unsqueeze(0))
         for g in range(2):
             nc.sync.dma_start(out=x_bb[:, g, :], in_=BB_feature[:, g, :])
-        load_scales(w_bb_scales, W_bbbb_scales)
         load_words(w_bb, W_bbbb_words)
+        load_scales(w_bb_scales, W_bbbb_scales)
         for g in range(2, FIRST_BATCH):
             nc.sync.dma_start(out=x_bb[:, g, :], in_=BB_feature[:, g, :])
         nc.sync.dma_start(out=x_rf[:], in_=RF_feature)
@@ -104,8 +107,7 @@ def tile_gnn_layer_pb_kernel(
             "v": v_rf[:],
             "m": m_rf[:],
         }
-        bb_batches = [bb_rows[:FIRST_BATCH]] + [bb_rows[first : first + BATCH] for first in range(FIRST_BATCH, GROUPS, BATCH)]
-        rows = bb_batches[0] + [rf_row] + bb_rows[FIRST_BATCH:]
+        rows = bb_rows[:FIRST_BATCH] + [rf_row] + bb_rows[FIRST_BATCH:]
 
         def transpose(row):
             words = row["x"].bitcast(F32)
@@ -119,11 +121,12 @@ def tile_gnn_layer_pb_kernel(
                 flipped_units.append(xt)
             return flipped_units
 
-        def regroup(flipped_units):
+        def regroup(flipped_units, on_scalar=False):
             grouped_units = []
             for xt in flipped_units:
                 grouped = work.tile([P, UNIT], BF16, align_bytes=64)
-                nc.vector.tensor_copy(
+                copy = nc.scalar.copy if on_scalar else nc.vector.tensor_copy
+                copy(
                     out=grouped[:].bitcast(F32).rearrange("p (c r u) -> p c r u", c=2, u=2),
                     in_=xt[:].rearrange("p c u r -> p c r u"),
                 )
@@ -163,6 +166,11 @@ def tile_gnn_layer_pb_kernel(
             cols = slice(h * N_HALF, (h + 1) * N_HALF)
             nc.vector.tensor_tensor(out=row["v"][:, cols], in0=accs[h][:], in1=row["bias"][:, cols], op=ALU.add)
 
+        def sigmoid(row):
+            nc.scalar.activation(out=row["m"], in_=row["v"], func=ACT.Sigmoid, scale=-1.0)
+
+        first_batch = [bb_rows[g] if g != "rf" else rf_row for g in BATCHES[0]]
+        nc.scalar.activation(out=warm[:], in_=ln_floor[:], func=ACT.Sigmoid)
         flipped_of = {0: transpose(rows[0]), 1: transpose(rows[1])}
         grouped_of = {0: regroup(flipped_of[0])}
         accs_of = {}
@@ -181,34 +189,54 @@ def tile_gnn_layer_pb_kernel(
             if i >= 1:
                 add_bias(rows[i - 1], accs_of[i - 1], 0)
             if i + 1 < len(rows):
-                grouped_of[i + 1] = regroup(flipped_of[i + 1])
+                grouped_of[i + 1] = regroup(flipped_of[i + 1], i + 1 in S_ROWS)
             if i >= 1:
                 add_bias(rows[i - 1], accs_of[i - 1], 1)
+                if rows[i - 1] in first_batch:
+                    sigmoid(rows[i - 1])
 
-        def sigmoid(batch):
-            for row in batch:
-                nc.scalar.activation(out=row["m"], in_=row["v"], func=ACT.Sigmoid, scale=-1.0)
-
-        batches = [bb_batches[0], [rf_row] + bb_batches[1]] + bb_batches[2:]
         halves = [slice(h * N_HALF, (h + 1) * N_HALF) for h in range(HALVES)]
-        sigmoid(batches[0])
+        by_name = {g: bb_rows[g] for g in range(GROUPS)}
+        by_name["rf"] = rf_row
+        batches = [[by_name[name] for name in names] for names in BATCHES]
+        def multiply_v(row, pieces):
+            for cols in pieces:
+                nc.vector.tensor_tensor(out=row["m"][:, cols], in0=row["m"][:, cols], in1=row["v"][:, cols], op=ALU.mult)
+
+        def add_rf(row, pieces):
+            for cols in pieces:
+                nc.vector.tensor_tensor(out=row["m"][:, cols], in0=row["m"][:, cols], in1=m_rf[:, cols], op=ALU.add)
+                nc.sync.dma_start(out=row["out"][:, cols], in_=row["m"][:, cols])
+
+        whole = [slice(0, DB)]
         lacking_rf = []
-        for b in range(len(batches)):
-            for row in batches[b]:
-                nc.scalar.activation(out=row["m"], in_=row["m"], func=ACT.Ln, bias=ln_floor[:])
-            if b + 1 < len(batches):
-                sigmoid(batches[b + 1])
-            for row in batches[b]:
-                nc.scalar.activation(out=row["m"], in_=row["m"], func=ACT.Tanh, scale=-1.0)
-                for cols in halves:
-                    nc.vector.tensor_tensor(out=row["m"][:, cols], in0=row["m"][:, cols], in1=row["v"][:, cols], op=ALU.mult)
-                if row is not rf_row:
-                    lacking_rf.append(row)
-                if b >= 1:
-                    for late in lacking_rf:
-                        for cols in halves:
-                            nc.vector.tensor_tensor(
-                                out=late["m"][:, cols], in0=late["m"][:, cols], in1=m_rf[:, cols], op=ALU.add
-                            )
-                            nc.sync.dma_start(out=late["out"][:, cols], in_=late["m"][:, cols])
-                    lacking_rf = []
+        rf_done = False
+        order = [(b, row) for b in range(len(batches)) for row in batches[b]]
+        for k, (b, row) in enumerate(order):
+            if row is batches[b][0]:
+                for r in batches[b]:
+                    nc.scalar.activation(out=r["m"], in_=r["m"], func=ACT.Ln, bias=ln_floor[:])
+                following = list(batches[b + 1]) if b + 1 < len(batches) else []
+            n = len(following) if row is batches[b][-1] else PER
+            front, following = following[:n], following[n:]
+            if row is batches[b][-1] and row is not batches[b][0]:
+                before, behind = front[:1], front[1:]
+            else:
+                before, behind = front, []
+            for later in before:
+                sigmoid(later)
+            last = k == len(order) - 1
+            for cols in halves if last else whole:
+                nc.scalar.activation(out=row["m"][:, cols], in_=row["m"][:, cols], func=ACT.Tanh, scale=-1.0)
+            for later in behind:
+                sigmoid(later)
+            multiply_v(row, halves if last else whole)
+            if rf_done:
+                while lacking_rf:
+                    add_rf(lacking_rf.pop(0), whole)
+            if row is rf_row:
+                rf_done = True
+            elif last:
+                add_rf(row, halves)
+            else:
+                lacking_rf.append(row)

@@ -21,8 +21,12 @@ N_HALF = 512
 HALVES = DB // N_HALF
 FIRST_BATCH = 3
 PER = 1
-S_ROWS = (1, 2, 3, 4)
-BATCHES = ((0, 1, 2), ("rf", 3, 4, 5, 6, 7, 8, 9, 10), (11, 12, 13, 14), (15,))
+S_ROWS = (2, 4)
+BATCHES = ((0, 1, 2), (3, 4, 5, 6, 7, 8, 9, 10, 11), (12, 13, 14, 15))
+RF_SIG = 1
+QUARTER = 256
+RF_SPREAD = 2
+S_PER = 2
 LN_FLOOR = 2.0**-60
 
 FLOPS = 2 * (P * GROUPS * DB * DB + P * DR * DB)
@@ -55,9 +59,10 @@ def tile_gnn_layer_pb_kernel(
         m_bb = keep.tile([P, GROUPS, DB], F32)
         v_rf = keep.tile([P, DB], F32)
         m_rf = keep.tile([P, DB], F32)
+        inv = keep.tile([P, 6, QUARTER], F32)
 
-        nc.vector.memset(w_bb_scales[:].bitcast(I32), 0)
         nc.vector.memset(bias_rows[:].bitcast(I32), 0)
+        nc.vector.memset(w_bb_scales[:].bitcast(I32), 0)
         nc.vector.memset(w_rf_scales[:].bitcast(I32), 0)
         nc.vector.memset(ln_floor[:], LN_FLOOR)
         make_identity(nc, identity[:])
@@ -73,15 +78,15 @@ def tile_gnn_layer_pb_kernel(
         def load_words(words_tile, words):
             nc.sync.dma_start(out=words_tile[:].bitcast(I32), in_=words.bitcast(I32).rearrange("c p n -> p c n"))
 
-        nc.scalar.dma_start(out=bias_rows[0:1, 0:DB], in_=b_bbbb.unsqueeze(0))
-        nc.scalar.dma_start(out=bias_rows[0:1, DB : 2 * DB], in_=b_rfbb.unsqueeze(0))
         for g in range(2):
             nc.sync.dma_start(out=x_bb[:, g, :], in_=BB_feature[:, g, :])
         load_words(w_bb, W_bbbb_words)
         load_scales(w_bb_scales, W_bbbb_scales)
+        nc.scalar.dma_start(out=bias_rows[0:1, 0:DB], in_=b_bbbb.unsqueeze(0))
         for g in range(2, FIRST_BATCH):
             nc.sync.dma_start(out=x_bb[:, g, :], in_=BB_feature[:, g, :])
         nc.sync.dma_start(out=x_rf[:], in_=RF_feature)
+        nc.sync.dma_start(out=bias_rows[0:1, DB : 2 * DB], in_=b_rfbb.unsqueeze(0))
         load_scales(w_rf_scales, W_rfbb_scales)
         load_words(w_rf, W_rfbb_words)
         for g in range(FIRST_BATCH, GROUPS):
@@ -166,77 +171,147 @@ def tile_gnn_layer_pb_kernel(
             cols = slice(h * N_HALF, (h + 1) * N_HALF)
             nc.vector.tensor_tensor(out=row["v"][:, cols], in0=accs[h][:], in1=row["bias"][:, cols], op=ALU.add)
 
-        def sigmoid(row):
-            nc.scalar.activation(out=row["m"], in_=row["v"], func=ACT.Sigmoid, scale=-1.0)
-
-        first_batch = [bb_rows[g] if g != "rf" else rf_row for g in BATCHES[0]]
         nc.scalar.activation(out=warm[:], in_=ln_floor[:], func=ACT.Sigmoid)
+        halves = [slice(h * N_HALF, (h + 1) * N_HALF) for h in range(HALVES)]
+        batches = [[bb_rows[g] for g in names] for names in BATCHES]
+
+        def multiply_v(row, cols):
+            nc.vector.tensor_tensor(out=row["m"][:, cols], in0=row["m"][:, cols], in1=row["v"][:, cols], op=ALU.mult)
+
+        def add_rf(row, pieces):
+            for cols in pieces:
+                nc.vector.scalar_tensor_tensor(
+                    out=row["m"][:, cols], in0=m_rf[:, cols], scalar=2.0, in1=row["m"][:, cols], op0=ALU.mult, op1=ALU.add
+                )
+                nc.sync.dma_start(out=row["out"][:, cols], in_=row["m"][:, cols])
+
+        def rf_steps():
+            q = [m_rf[:, i * QUARTER : (i + 1) * QUARTER] for i in range(4)]
+            v = [v_rf[:, i * QUARTER : (i + 1) * QUARTER] for i in range(4)]
+            p01, p23, p, i01, i23, t = [inv[:, i, :] for i in range(6)]
+
+            def mul(o, x, y):
+                return lambda: nc.vector.tensor_tensor(out=o, in0=x, in1=y, op=ALU.mult)
+
+            def plus_one(cols):
+                return lambda: nc.vector.tensor_scalar(
+                    out=m_rf[:, cols], in0=m_rf[:, cols], scalar1=1.0, scalar2=None, op0=ALU.add
+                )
+
+            def last(i, x):
+                return lambda: nc.vector.scalar_tensor_tensor(
+                    out=q[i], in0=x, scalar=0.5, in1=v[i], op0=ALU.subtract, op1=ALU.mult
+                )
+
+            return [
+                plus_one(halves[0]),
+                plus_one(halves[1]),
+                mul(p01, q[0], q[1]),
+                mul(p23, q[2], q[3]),
+                None,
+                mul(p, p01, p23),
+                None,
+                lambda: nc.vector.reciprocal(out=t, in_=p),
+                None,
+                mul(i01, t, p23),
+                mul(i23, t, p01),
+                mul(p, i01, q[1]),
+                mul(p23, i23, q[3]),
+                mul(p01, i01, q[0]),
+                mul(t, i23, q[2]),
+                last(0, p),
+                last(2, p23),
+                last(1, p01),
+                last(3, t),
+            ]
+
+        def scalar_items():
+            items = [("sigmoid", row) for row in batches[0]]
+            for b, batch in enumerate(batches):
+                items += [("log", row) for row in batch]
+                following = list(batches[b + 1]) if b + 1 < len(batches) else []
+                if b == 0:
+                    following.insert(RF_SIG, rf_row)
+                for k, row in enumerate(batch):
+                    n = len(following) if k == len(batch) - 1 else PER
+                    front, following = following[:n], following[n:]
+                    items += [("sigmoid", later) for later in front[:1]]
+                    items.append(("tanh", row))
+                    items += [("sigmoid", later) for later in front[1:]]
+            return items
+
+        items = scalar_items()
+        last_row = batches[-1][-1]
+        made = []
+
+        def run_scalar(n):
+            while n > 0 and items:
+                kind, row = items[0]
+                if kind == "sigmoid" and row not in made:
+                    return
+                items.pop(0)
+                n -= 1
+                m = row["m"]
+                if kind == "sigmoid":
+                    nc.scalar.activation(out=m, in_=row["v"], func=ACT.Sigmoid, scale=-1.0)
+                    if row is rf_row:
+                        nc.scalar.activation(out=m, in_=m, func=ACT.Square)
+                elif kind == "log":
+                    nc.scalar.activation(out=m, in_=m, func=ACT.Ln, bias=ln_floor[:])
+                else:
+                    for cols in halves if row is last_row else [slice(0, DB)]:
+                        nc.scalar.activation(out=m[:, cols], in_=m[:, cols], func=ACT.Tanh, scale=-1.0)
+
         flipped_of = {0: transpose(rows[0]), 1: transpose(rows[1])}
         grouped_of = {0: regroup(flipped_of[0])}
         accs_of = {}
 
-        for j in range(2 * HALVES):
-            cols = slice(j * N_HALF, (j + 1) * N_HALF)
-            spread = sums.tile([P, N_HALF], F32, tag="acc")
-            nc.tensor.matmul(out=spread[:], lhsT=ones[:], rhs=bias_rows[:, cols], start=True, stop=True)
-            nc.scalar.copy(out=bias[:, cols], in_=spread[:])
+        def spread_bias(first):
+            for j in range(first, first + HALVES):
+                cols = slice(j * N_HALF, (j + 1) * N_HALF)
+                spread = sums.tile([P, N_HALF], F32, tag="acc")
+                nc.tensor.matmul(out=spread[:], lhsT=ones[:], rhs=bias_rows[:, cols], start=True, stop=True)
+                nc.scalar.copy(out=bias[:, cols], in_=spread[:])
 
+        spread_bias(0)
         for i in range(len(rows) + 1):
+            if i == RF_SPREAD:
+                spread_bias(HALVES)
             if i < len(rows):
                 accs_of[i] = multiply(rows[i], quantise(grouped_of[i]))
             if i + 2 < len(rows):
                 flipped_of[i + 2] = transpose(rows[i + 2])
             if i >= 1:
                 add_bias(rows[i - 1], accs_of[i - 1], 0)
-            if i + 1 < len(rows):
-                grouped_of[i + 1] = regroup(flipped_of[i + 1], i + 1 in S_ROWS)
+            if i + 1 < len(rows) and i + 1 not in S_ROWS:
+                grouped_of[i + 1] = regroup(flipped_of[i + 1])
             if i >= 1:
                 add_bias(rows[i - 1], accs_of[i - 1], 1)
-                if rows[i - 1] in first_batch:
-                    sigmoid(rows[i - 1])
+                made.append(rows[i - 1])
+                run_scalar(S_PER if i - 1 >= len(batches[0]) else 1)
+            if i + 2 in S_ROWS:
+                grouped_of[i + 2] = regroup(flipped_of[i + 2], True)
+        run_scalar(len(items))
 
-        halves = [slice(h * N_HALF, (h + 1) * N_HALF) for h in range(HALVES)]
-        by_name = {g: bb_rows[g] for g in range(GROUPS)}
-        by_name["rf"] = rf_row
-        batches = [[by_name[name] for name in names] for names in BATCHES]
-        def multiply_v(row, pieces):
-            for cols in pieces:
-                nc.vector.tensor_tensor(out=row["m"][:, cols], in0=row["m"][:, cols], in1=row["v"][:, cols], op=ALU.mult)
-
-        def add_rf(row, pieces):
-            for cols in pieces:
-                nc.vector.tensor_tensor(out=row["m"][:, cols], in0=row["m"][:, cols], in1=m_rf[:, cols], op=ALU.add)
-                nc.sync.dma_start(out=row["out"][:, cols], in_=row["m"][:, cols])
-
-        whole = [slice(0, DB)]
-        lacking_rf = []
-        rf_done = False
-        order = [(b, row) for b in range(len(batches)) for row in batches[b]]
-        for k, (b, row) in enumerate(order):
-            if row is batches[b][0]:
-                for r in batches[b]:
-                    nc.scalar.activation(out=r["m"], in_=r["m"], func=ACT.Ln, bias=ln_floor[:])
-                following = list(batches[b + 1]) if b + 1 < len(batches) else []
-            n = len(following) if row is batches[b][-1] else PER
-            front, following = following[:n], following[n:]
-            if row is batches[b][-1] and row is not batches[b][0]:
-                before, behind = front[:1], front[1:]
+        first = [(row, cols) for row in batches[0] for cols in halves]
+        while len(first) > 3:
+            multiply_v(*first.pop(0))
+        for step in rf_steps():
+            if step is None:
+                multiply_v(*first.pop(0))
             else:
-                before, behind = front, []
-            for later in before:
-                sigmoid(later)
-            last = k == len(order) - 1
-            for cols in halves if last else whole:
-                nc.scalar.activation(out=row["m"][:, cols], in_=row["m"][:, cols], func=ACT.Tanh, scale=-1.0)
-            for later in behind:
-                sigmoid(later)
-            multiply_v(row, halves if last else whole)
-            if rf_done:
+                step()
+        whole = [slice(0, DB)]
+        lacking_rf = list(batches[0])
+        for row in [r for batch in batches[1:] for r in batch]:
+            if row is last_row:
                 while lacking_rf:
                     add_rf(lacking_rf.pop(0), whole)
-            if row is rf_row:
-                rf_done = True
-            elif last:
+                for cols in halves:
+                    multiply_v(row, cols)
                 add_rf(row, halves)
             else:
+                while len(lacking_rf) > 1:
+                    add_rf(lacking_rf.pop(0), whole)
+                multiply_v(row, whole[0])
                 lacking_rf.append(row)

@@ -21,8 +21,9 @@ N_HALF = 512
 HALVES = DB // N_HALF
 FIRST_BATCH = 3
 PER = 1
+WARM_UPS = 5
 S_ROWS = (2, 4)
-BATCHES = ((0, 1, 2), (3, 4, 5, 6, 7, 8, 9, 10, 11), (12, 13, 14, 15))
+BATCHES = ((0, 1, 2), (3, 4, 5, 6, 7, 8, 9, 10, 11), (12, 13, 14), (15,))
 RF_SIG = 1
 QUARTER = 256
 RF_SPREAD = 2
@@ -55,12 +56,14 @@ def tile_gnn_layer_pb_kernel(
         bias = keep.tile([P, 2 * DB], F32)
         ln_floor = keep.tile([P, 1], F32)
         warm = keep.tile([P, 1], F32)
+        zeros = keep.tile([P, N_HALF], BF16)
         v_bb = keep.tile([P, GROUPS, DB], F32)
         m_bb = keep.tile([P, GROUPS, DB], F32)
         v_rf = keep.tile([P, DB], F32)
         m_rf = keep.tile([P, DB], F32)
         inv = keep.tile([P, 6, QUARTER], F32)
 
+        nc.vector.memset(zeros[:].bitcast(I32), 0)
         nc.vector.memset(bias_rows[:].bitcast(I32), 0)
         nc.vector.memset(w_bb_scales[:].bitcast(I32), 0)
         nc.vector.memset(w_rf_scales[:].bitcast(I32), 0)
@@ -262,6 +265,9 @@ def tile_gnn_layer_pb_kernel(
                     for cols in halves if row is last_row else [slice(0, DB)]:
                         nc.scalar.activation(out=m[:, cols], in_=m[:, cols], func=ACT.Tanh, scale=-1.0)
 
+        warm_up = sums.tile([P, N_HALF], F32, tag="acc")
+        for _ in range(WARM_UPS):
+            nc.tensor.matmul(out=warm_up[:], lhsT=zeros[:, 0:P], rhs=zeros[:], start=True, stop=True)
         flipped_of = {0: transpose(rows[0]), 1: transpose(rows[1])}
         grouped_of = {0: regroup(flipped_of[0])}
         accs_of = {}

@@ -19,14 +19,22 @@ K_PASS = 512
 UNIT = 2 * K_PASS
 N_HALF = 512
 HALVES = DB // N_HALF
-FIRST_BATCH = 3
 PER = 1
-WARM_UPS = 5
-S_ROWS = (2, 4)
+RF_ROW = 8
+WARM_UPS = 6
+S_ROWS = (2,)
 BATCHES = ((0, 1, 2), (3, 4, 5, 6, 7, 8, 9, 10, 11), (12, 13, 14), (15,))
-RF_SIG = 1
-QUARTER = 256
-RF_SPREAD = 2
+RF_SIG = 5
+LEVELS = 3
+SPLIT = 1
+RF_BATCH = 0
+ADD_FIRST = (2, 3)
+ADD_N = 2
+TAIL = 4
+SQ_V = 0
+FILL_FROM = 14
+FILL = 1
+RF_BIAS_AT = 12
 S_PER = 2
 LN_FLOOR = 2.0**-60
 
@@ -52,8 +60,9 @@ def tile_gnn_layer_pb_kernel(
         w_rf_scales = keep.tile([P, DR // K_PASS, DB], U8, align_bytes=64)
         identity = keep.tile([P, P], F32)
         ones = keep.tile([P, P], BF16)
-        bias_rows = keep.tile([P, 2 * DB], BF16)
-        bias = keep.tile([P, 2 * DB], F32)
+        bias_rows = keep.tile([P, DB], BF16)
+        rf_bias = keep.tile([P, DB], BF16)
+        bias = keep.tile([P, DB], F32)
         ln_floor = keep.tile([P, 1], F32)
         warm = keep.tile([P, 1], F32)
         zeros = keep.tile([P, N_HALF], BF16)
@@ -61,7 +70,7 @@ def tile_gnn_layer_pb_kernel(
         m_bb = keep.tile([P, GROUPS, DB], F32)
         v_rf = keep.tile([P, DB], F32)
         m_rf = keep.tile([P, DB], F32)
-        inv = keep.tile([P, 6, QUARTER], F32)
+        inv = keep.tile([P, 5 * N_HALF], F32)
 
         nc.vector.memset(zeros[:].bitcast(I32), 0)
         nc.vector.memset(bias_rows[:].bitcast(I32), 0)
@@ -86,13 +95,14 @@ def tile_gnn_layer_pb_kernel(
         load_words(w_bb, W_bbbb_words)
         load_scales(w_bb_scales, W_bbbb_scales)
         nc.scalar.dma_start(out=bias_rows[0:1, 0:DB], in_=b_bbbb.unsqueeze(0))
-        for g in range(2, FIRST_BATCH):
+        for g in range(2, RF_ROW):
             nc.sync.dma_start(out=x_bb[:, g, :], in_=BB_feature[:, g, :])
         nc.sync.dma_start(out=x_rf[:], in_=RF_feature)
-        nc.sync.dma_start(out=bias_rows[0:1, DB : 2 * DB], in_=b_rfbb.unsqueeze(0))
         load_scales(w_rf_scales, W_rfbb_scales)
         load_words(w_rf, W_rfbb_words)
-        for g in range(FIRST_BATCH, GROUPS):
+        for g in range(RF_ROW, GROUPS):
+            if g == RF_BIAS_AT:
+                nc.sync.dma_start(out=rf_bias[:], in_=b_rfbb.partition_broadcast(P))
             nc.sync.dma_start(out=x_bb[:, g, :], in_=BB_feature[:, g, :])
 
         bb_rows = [
@@ -100,7 +110,7 @@ def tile_gnn_layer_pb_kernel(
                 "x": x_bb[:, g, :],
                 "w": w_bb,
                 "w_scales": w_bb_scales,
-                "bias": bias[:, 0:DB],
+                "bias": bias[:],
                 "v": v_bb[:, g, :],
                 "m": m_bb[:, g, :],
                 "out": out[:, g, :],
@@ -111,11 +121,11 @@ def tile_gnn_layer_pb_kernel(
             "x": x_rf[:],
             "w": w_rf,
             "w_scales": w_rf_scales,
-            "bias": bias[:, DB : 2 * DB],
+            "bias": rf_bias[:],
             "v": v_rf[:],
             "m": m_rf[:],
         }
-        rows = bb_rows[:FIRST_BATCH] + [rf_row] + bb_rows[FIRST_BATCH:]
+        rows = bb_rows[:RF_ROW] + [rf_row] + bb_rows[RF_ROW:]
 
         def transpose(row):
             words = row["x"].bitcast(F32)
@@ -189,51 +199,60 @@ def tile_gnn_layer_pb_kernel(
                 nc.sync.dma_start(out=row["out"][:, cols], in_=row["m"][:, cols])
 
         def rf_steps():
-            q = [m_rf[:, i * QUARTER : (i + 1) * QUARTER] for i in range(4)]
-            v = [v_rf[:, i * QUARTER : (i + 1) * QUARTER] for i in range(4)]
-            p01, p23, p, i01, i23, t = [inv[:, i, :] for i in range(6)]
+            g = [m_rf[:, cols] for cols in halves]
+            v = [v_rf[:, cols] for cols in halves]
+            d1 = inv[:, 0:N_HALF]
+            widths = [N_HALF >> level for level in range(1 + LEVELS)]
+            products = [inv[:, N_HALF : 2 * N_HALF]]
+            first = 2 * N_HALF
+            for width in widths[1:]:
+                products.append(inv[:, first : first + width])
+                first += width
+            inverses = []
+            for width in widths:
+                inverses.append(inv[:, first : first + width])
+                first += width
+            steps = []
 
             def mul(o, x, y):
-                return lambda: nc.vector.tensor_tensor(out=o, in0=x, in1=y, op=ALU.mult)
+                steps.append(lambda: nc.vector.tensor_tensor(out=o, in0=x, in1=y, op=ALU.mult))
 
-            def plus_one(cols):
-                return lambda: nc.vector.tensor_scalar(
-                    out=m_rf[:, cols], in0=m_rf[:, cols], scalar1=1.0, scalar2=None, op0=ALU.add
+            def plus_one_times(o, x, y):
+                steps.append(
+                    lambda: nc.vector.scalar_tensor_tensor(out=o, in0=x, scalar=1.0, in1=y, op0=ALU.add, op1=ALU.mult)
                 )
 
-            def last(i, x):
-                return lambda: nc.vector.scalar_tensor_tensor(
-                    out=q[i], in0=x, scalar=0.5, in1=v[i], op0=ALU.subtract, op1=ALU.mult
+            def minus_half_times(o, x, y):
+                steps.append(
+                    lambda: nc.vector.scalar_tensor_tensor(out=o, in0=x, scalar=0.5, in1=y, op0=ALU.subtract, op1=ALU.mult)
                 )
 
-            return [
-                plus_one(halves[0]),
-                plus_one(halves[1]),
-                mul(p01, q[0], q[1]),
-                mul(p23, q[2], q[3]),
-                None,
-                mul(p, p01, p23),
-                None,
-                lambda: nc.vector.reciprocal(out=t, in_=p),
-                None,
-                mul(i01, t, p23),
-                mul(i23, t, p01),
-                mul(p, i01, q[1]),
-                mul(p23, i23, q[3]),
-                mul(p01, i01, q[0]),
-                mul(t, i23, q[2]),
-                last(0, p),
-                last(2, p23),
-                last(1, p01),
-                last(3, t),
-            ]
+            if SQ_V:
+                mul(g[1], g[1], g[1])
+                mul(g[0], g[0], g[0])
+            steps.append(lambda: nc.vector.tensor_scalar(out=d1, in0=g[1], scalar1=1.0, scalar2=None, op0=ALU.add))
+            plus_one_times(products[0], g[0], d1)
+            for level in range(LEVELS):
+                width = widths[level + 1]
+                mul(products[level + 1], products[level][:, 0:width], products[level][:, width : 2 * width])
+            steps.append(lambda: nc.vector.reciprocal(out=inverses[LEVELS], in_=products[LEVELS]))
+            for level in range(LEVELS - 1, -1, -1):
+                width = widths[level + 1]
+                low, high = slice(0, width), slice(width, 2 * width)
+                mul(inverses[level][:, low], inverses[level + 1], products[level][:, high])
+                mul(inverses[level][:, high], inverses[level + 1], products[level][:, low])
+            mul(d1, inverses[0], d1)
+            plus_one_times(inverses[0], g[0], inverses[0])
+            minus_half_times(g[0], d1, v[0])
+            minus_half_times(g[1], inverses[0], v[1])
+            return steps
 
         def scalar_items():
             items = [("sigmoid", row) for row in batches[0]]
             for b, batch in enumerate(batches):
-                items += [("log", row) for row in batch]
+                items.append(("log", batch))
                 following = list(batches[b + 1]) if b + 1 < len(batches) else []
-                if b == 0:
+                if b == RF_BATCH:
                     following.insert(RF_SIG, rf_row)
                 for k, row in enumerate(batch):
                     n = len(following) if k == len(batch) - 1 else PER
@@ -245,7 +264,25 @@ def tile_gnn_layer_pb_kernel(
 
         items = scalar_items()
         last_row = batches[-1][-1]
+        last_pieces = [slice(i * DB // TAIL, (i + 1) * DB // TAIL) for i in range(TAIL)]
+        split = [batches[0][-1], batches[1][-1]] if SPLIT else []
+
+        def names_of(batch):
+            b = batches.index(batch)
+            return BATCHES[b][0], len(BATCHES[b])
+
         made = []
+        done = []
+        first_tiles = [(row, cols) for row in batches[0] for cols in halves]
+        rf_work = rf_steps()
+
+        def fill(n):
+            for _ in range(n):
+                if rf_work and ("sigmoid", rf_row) in done:
+                    rf_work.pop(0)()
+                elif first_tiles and ("tanh", first_tiles[0][0]) in done:
+                    multiply_v(*first_tiles.pop(0))
+
 
         def run_scalar(n):
             while n > 0 and items:
@@ -254,16 +291,21 @@ def tile_gnn_layer_pb_kernel(
                     return
                 items.pop(0)
                 n -= 1
-                m = row["m"]
-                if kind == "sigmoid":
-                    nc.scalar.activation(out=m, in_=row["v"], func=ACT.Sigmoid, scale=-1.0)
-                    if row is rf_row:
-                        nc.scalar.activation(out=m, in_=m, func=ACT.Square)
-                elif kind == "log":
+                if kind == "log":
+                    first, count = names_of(row)
+                    m = m_bb[:, first : first + count, :]
                     nc.scalar.activation(out=m, in_=m, func=ACT.Ln, bias=ln_floor[:])
+                elif kind == "sigmoid":
+                    m, v = row["m"], row["v"]
+                    for cols in halves if row in split else [slice(0, DB)]:
+                        nc.scalar.activation(out=m[:, cols], in_=v[:, cols], func=ACT.Sigmoid, scale=-1.0)
+                    if row is rf_row and not SQ_V:
+                        nc.scalar.activation(out=m, in_=m, func=ACT.Square)
                 else:
-                    for cols in halves if row is last_row else [slice(0, DB)]:
+                    m = row["m"]
+                    for cols in last_pieces if row is last_row else [slice(0, DB)]:
                         nc.scalar.activation(out=m[:, cols], in_=m[:, cols], func=ACT.Tanh, scale=-1.0)
+                done.append((kind, row))
 
         warm_up = sums.tile([P, N_HALF], F32, tag="acc")
         for _ in range(WARM_UPS):
@@ -272,50 +314,60 @@ def tile_gnn_layer_pb_kernel(
         grouped_of = {0: regroup(flipped_of[0])}
         accs_of = {}
 
-        def spread_bias(first):
-            for j in range(first, first + HALVES):
+        def spread_bias():
+            for j in range(HALVES):
                 cols = slice(j * N_HALF, (j + 1) * N_HALF)
                 spread = sums.tile([P, N_HALF], F32, tag="acc")
                 nc.tensor.matmul(out=spread[:], lhsT=ones[:], rhs=bias_rows[:, cols], start=True, stop=True)
                 nc.scalar.copy(out=bias[:, cols], in_=spread[:])
 
-        spread_bias(0)
+        spread_bias()
+        def finish_row(i, h):
+            add_bias(rows[i], accs_of[i], h)
+            if h == HALVES - 1:
+                made.append(rows[i])
+
         for i in range(len(rows) + 1):
-            if i == RF_SPREAD:
-                spread_bias(HALVES)
+            filling = FILL if i >= FILL_FROM else 0
+            steps = [(i - 1, h) for h in range(HALVES)] if i >= 1 else []
+            if i in ADD_FIRST:
+                for step in steps[:ADD_N]:
+                    finish_row(*step)
+                steps = steps[ADD_N:]
+                if not steps:
+                    run_scalar(1)
             if i < len(rows):
                 accs_of[i] = multiply(rows[i], quantise(grouped_of[i]))
             if i + 2 < len(rows):
                 flipped_of[i + 2] = transpose(rows[i + 2])
-            if i >= 1:
-                add_bias(rows[i - 1], accs_of[i - 1], 0)
+            fill(filling)
+            if len(steps) == HALVES:
+                finish_row(*steps.pop(0))
+                fill(filling)
             if i + 1 < len(rows) and i + 1 not in S_ROWS:
                 grouped_of[i + 1] = regroup(flipped_of[i + 1])
+                fill(filling)
+            if steps:
+                finish_row(*steps.pop(0))
+                fill(filling)
             if i >= 1:
-                add_bias(rows[i - 1], accs_of[i - 1], 1)
-                made.append(rows[i - 1])
                 run_scalar(S_PER if i - 1 >= len(batches[0]) else 1)
             if i + 2 in S_ROWS:
                 grouped_of[i + 2] = regroup(flipped_of[i + 2], True)
         run_scalar(len(items))
 
-        first = [(row, cols) for row in batches[0] for cols in halves]
-        while len(first) > 3:
-            multiply_v(*first.pop(0))
-        for step in rf_steps():
-            if step is None:
-                multiply_v(*first.pop(0))
-            else:
-                step()
+        fill(len(rf_work) + len(first_tiles))
         whole = [slice(0, DB)]
         lacking_rf = list(batches[0])
         for row in [r for batch in batches[1:] for r in batch]:
             if row is last_row:
                 while lacking_rf:
                     add_rf(lacking_rf.pop(0), whole)
-                for cols in halves:
+                for i, cols in enumerate(last_pieces):
                     multiply_v(row, cols)
-                add_rf(row, halves)
+                    if i >= 1:
+                        add_rf(row, last_pieces[i - 1 : i])
+                add_rf(row, last_pieces[-1:])
             else:
                 while len(lacking_rf) > 1:
                     add_rf(lacking_rf.pop(0), whole)

import concourse.mybir as mybir
from concourse.masks import make_identity

F32 = mybir.dt.float32
BF16 = mybir.dt.bfloat16
I32 = mybir.dt.int32
U32 = mybir.dt.uint32
U8 = mybir.dt.uint8
FP8X4 = mybir.dt.float8_e4m3fn_x4
FP4X4 = mybir.dt.float4_e2m1fn_x4
ACT = mybir.ActivationFunctionType
ALU = mybir.AluOpType

P = 128
GROUPS = 16
DB = 1024
DR = 2048
K_PASS = 512
UNIT = 2 * K_PASS
N_HALF = 512
HALVES = DB // N_HALF
PER = 1
RF_ROW = 8
WARM_UPS = 6
S_ROWS = (2,)
BATCHES = ((0, 1, 2), (3, 4, 5, 6, 7, 8, 9, 10, 11), (12, 13, 14), (15,))
RF_SIG = 5
LEVELS = 3
SPLIT = 1
RF_BATCH = 0
ADD_FIRST = (2, 3)
ADD_N = 2
TAIL = 4
SQ_V = 0
FILL_FROM = 14
FILL = 1
RF_BIAS_AT = 12
S_PER = 2
LN_FLOOR = 2.0**-60

FLOPS = 2 * (P * GROUPS * DB * DB + P * DR * DB)


def tile_gnn_layer_pb_kernel(
    tc, BB_feature, RF_feature, W_bbbb_words, W_bbbb_scales, b_bbbb, W_rfbb_words, W_rfbb_scales, b_rfbb, out
):
    nc = tc.nc
    with (
        tc.tile_pool(name="keep", bufs=1) as keep,
        tc.tile_pool(name="work", bufs=4) as work,
        tc.psum_pool(name="flipped", bufs=3) as flipped,
        tc.psum_pool(name="sums", bufs=4) as sums,
        tc.manual_schedule(),
    ):
        x_bb = keep.tile([P, GROUPS, DB], BF16)
        x_rf = keep.tile([P, DR], BF16)
        w_bb = keep.tile([P, DB // K_PASS, 2 * DB], U8, align_bytes=64)
        w_rf = keep.tile([P, DR // K_PASS, 2 * DB], U8, align_bytes=64)
        w_bb_scales = keep.tile([P, DB // K_PASS, DB], U8, align_bytes=64)
        w_rf_scales = keep.tile([P, DR // K_PASS, DB], U8, align_bytes=64)
        identity = keep.tile([P, P], F32)
        ones = keep.tile([P, P], BF16)
        bias_rows = keep.tile([P, DB], BF16)
        rf_bias = keep.tile([P, DB], BF16)
        bias = keep.tile([P, DB], F32)
        ln_floor = keep.tile([P, 1], F32)
        warm = keep.tile([P, 1], F32)
        zeros = keep.tile([P, N_HALF], BF16)
        v_bb = keep.tile([P, GROUPS, DB], F32)
        m_bb = keep.tile([P, GROUPS, DB], F32)
        v_rf = keep.tile([P, DB], F32)
        m_rf = keep.tile([P, DB], F32)
        inv = keep.tile([P, 5 * N_HALF], F32)

        nc.vector.memset(zeros[:].bitcast(I32), 0)
        nc.vector.memset(bias_rows[:].bitcast(I32), 0)
        nc.vector.memset(w_bb_scales[:].bitcast(I32), 0)
        nc.vector.memset(w_rf_scales[:].bitcast(I32), 0)
        nc.vector.memset(ln_floor[:], LN_FLOOR)
        make_identity(nc, identity[:])
        nc.gpsimd.memset(ones[:], 1.0)

        def load_scales(planes, scales):
            for r in range(4):
                nc.sync.dma_start(
                    out=planes[r:P:32, :, :].bitcast(I32),
                    in_=scales.bitcast(I32)[:, r:16:4, :].rearrange("c q n -> q c n"),
                )

        def load_words(words_tile, words):
            nc.sync.dma_start(out=words_tile[:].bitcast(I32), in_=words.bitcast(I32).rearrange("c p n -> p c n"))

        for g in range(2):
            nc.sync.dma_start(out=x_bb[:, g, :], in_=BB_feature[:, g, :])
        load_words(w_bb, W_bbbb_words)
        load_scales(w_bb_scales, W_bbbb_scales)
        nc.scalar.dma_start(out=bias_rows[0:1, 0:DB], in_=b_bbbb.unsqueeze(0))
        for g in range(2, RF_ROW):
            nc.sync.dma_start(out=x_bb[:, g, :], in_=BB_feature[:, g, :])
        nc.sync.dma_start(out=x_rf[:], in_=RF_feature)
        load_scales(w_rf_scales, W_rfbb_scales)
        load_words(w_rf, W_rfbb_words)
        for g in range(RF_ROW, GROUPS):
            if g == RF_BIAS_AT:
                nc.sync.dma_start(out=rf_bias[:], in_=b_rfbb.partition_broadcast(P))
            nc.sync.dma_start(out=x_bb[:, g, :], in_=BB_feature[:, g, :])

        bb_rows = [
            {
                "x": x_bb[:, g, :],
                "w": w_bb,
                "w_scales": w_bb_scales,
                "bias": bias[:],
                "v": v_bb[:, g, :],
                "m": m_bb[:, g, :],
                "out": out[:, g, :],
            }
            for g in range(GROUPS)
        ]
        rf_row = {
            "x": x_rf[:],
            "w": w_rf,
            "w_scales": w_rf_scales,
            "bias": rf_bias[:],
            "v": v_rf[:],
            "m": m_rf[:],
        }
        rows = bb_rows[:RF_ROW] + [rf_row] + bb_rows[RF_ROW:]

        def transpose(row):
            words = row["x"].bitcast(F32)
            flipped_units = []
            for unit in range(words.shape[1] * 2 // UNIT):
                xt = flipped.tile([P, 2, 2, P], F32)
                for c in range(2):
                    for u in range(2):
                        first = (2 * unit + c) * (K_PASS // 2)
                        nc.tensor.transpose(xt[:, c, u, :], words[:, first + u : first + K_PASS // 2 : 2], identity[:])
                flipped_units.append(xt)
            return flipped_units

        def regroup(flipped_units, on_scalar=False):
            grouped_units = []
            for xt in flipped_units:
                grouped = work.tile([P, UNIT], BF16, align_bytes=64)
                copy = nc.scalar.copy if on_scalar else nc.vector.tensor_copy
                copy(
                    out=grouped[:].bitcast(F32).rearrange("p (c r u) -> p c r u", c=2, u=2),
                    in_=xt[:].rearrange("p c u r -> p c r u"),
                )
                grouped_units.append(grouped)
            return grouped_units

        def quantise(grouped_units):
            quantised_units = []
            for grouped in grouped_units:
                codes = work.tile([P, 2 * P], U32, align_bytes=64)
                scales = work.tile([P, 2 * P], U8, align_bytes=64)
                nc.vector.quantize_mx(out=codes[:].bitcast(FP8X4), scales=scales[:], in_=grouped[:])
                quantised_units.append((codes, scales))
            return quantised_units

        def multiply(row, quantised_units):
            passes = 2 * len(quantised_units)
            accs = []
            for h in range(HALVES):
                acc = sums.tile([P, N_HALF], F32)
                for c in range(passes):
                    codes, scales = quantised_units[c // 2]
                    x_cols = slice((c % 2) * P, (c % 2 + 1) * P)
                    nc.tensor.matmul_mx(
                        out=acc[:],
                        lhsT=codes[:, x_cols].bitcast(FP8X4),
                        lhsT_scale=scales[:, x_cols],
                        rhs=row["w"][:, c, 2 * h * N_HALF : 2 * (h + 1) * N_HALF].bitcast(FP4X4),
                        rhs_scale=row["w_scales"][:, c, h * N_HALF : (h + 1) * N_HALF],
                        start=(c == 0),
                        stop=(c == passes - 1),
                    )
                accs.append(acc)
            return accs

        def add_bias(row, accs, h):
            cols = slice(h * N_HALF, (h + 1) * N_HALF)
            nc.vector.tensor_tensor(out=row["v"][:, cols], in0=accs[h][:], in1=row["bias"][:, cols], op=ALU.add)

        nc.scalar.activation(out=warm[:], in_=ln_floor[:], func=ACT.Sigmoid)
        halves = [slice(h * N_HALF, (h + 1) * N_HALF) for h in range(HALVES)]
        batches = [[bb_rows[g] for g in names] for names in BATCHES]

        def multiply_v(row, cols):
            nc.vector.tensor_tensor(out=row["m"][:, cols], in0=row["m"][:, cols], in1=row["v"][:, cols], op=ALU.mult)

        def add_rf(row, pieces):
            for cols in pieces:
                nc.vector.scalar_tensor_tensor(
                    out=row["m"][:, cols], in0=m_rf[:, cols], scalar=2.0, in1=row["m"][:, cols], op0=ALU.mult, op1=ALU.add
                )
                nc.sync.dma_start(out=row["out"][:, cols], in_=row["m"][:, cols])

        def rf_steps():
            g = [m_rf[:, cols] for cols in halves]
            v = [v_rf[:, cols] for cols in halves]
            d1 = inv[:, 0:N_HALF]
            widths = [N_HALF >> level for level in range(1 + LEVELS)]
            products = [inv[:, N_HALF : 2 * N_HALF]]
            first = 2 * N_HALF
            for width in widths[1:]:
                products.append(inv[:, first : first + width])
                first += width
            inverses = []
            for width in widths:
                inverses.append(inv[:, first : first + width])
                first += width
            steps = []

            def mul(o, x, y):
                steps.append(lambda: nc.vector.tensor_tensor(out=o, in0=x, in1=y, op=ALU.mult))

            def plus_one_times(o, x, y):
                steps.append(
                    lambda: nc.vector.scalar_tensor_tensor(out=o, in0=x, scalar=1.0, in1=y, op0=ALU.add, op1=ALU.mult)
                )

            def minus_half_times(o, x, y):
                steps.append(
                    lambda: nc.vector.scalar_tensor_tensor(out=o, in0=x, scalar=0.5, in1=y, op0=ALU.subtract, op1=ALU.mult)
                )

            if SQ_V:
                mul(g[1], g[1], g[1])
                mul(g[0], g[0], g[0])
            steps.append(lambda: nc.vector.tensor_scalar(out=d1, in0=g[1], scalar1=1.0, scalar2=None, op0=ALU.add))
            plus_one_times(products[0], g[0], d1)
            for level in range(LEVELS):
                width = widths[level + 1]
                mul(products[level + 1], products[level][:, 0:width], products[level][:, width : 2 * width])
            steps.append(lambda: nc.vector.reciprocal(out=inverses[LEVELS], in_=products[LEVELS]))
            for level in range(LEVELS - 1, -1, -1):
                width = widths[level + 1]
                low, high = slice(0, width), slice(width, 2 * width)
                mul(inverses[level][:, low], inverses[level + 1], products[level][:, high])
                mul(inverses[level][:, high], inverses[level + 1], products[level][:, low])
            mul(d1, inverses[0], d1)
            plus_one_times(inverses[0], g[0], inverses[0])
            minus_half_times(g[0], d1, v[0])
            minus_half_times(g[1], inverses[0], v[1])
            return steps

        def scalar_items():
            items = [("sigmoid", row) for row in batches[0]]
            for b, batch in enumerate(batches):
                items.append(("log", batch))
                following = list(batches[b + 1]) if b + 1 < len(batches) else []
                if b == RF_BATCH:
                    following.insert(RF_SIG, rf_row)
                for k, row in enumerate(batch):
                    n = len(following) if k == len(batch) - 1 else PER
                    front, following = following[:n], following[n:]
                    items += [("sigmoid", later) for later in front[:1]]
                    items.append(("tanh", row))
                    items += [("sigmoid", later) for later in front[1:]]
            return items

        items = scalar_items()
        last_row = batches[-1][-1]
        last_pieces = [slice(i * DB // TAIL, (i + 1) * DB // TAIL) for i in range(TAIL)]
        split = [batches[0][-1], batches[1][-1]] if SPLIT else []

        def names_of(batch):
            b = batches.index(batch)
            return BATCHES[b][0], len(BATCHES[b])

        made = []
        done = []
        first_tiles = [(row, cols) for row in batches[0] for cols in halves]
        rf_work = rf_steps()

        def fill(n):
            for _ in range(n):
                if rf_work and ("sigmoid", rf_row) in done:
                    rf_work.pop(0)()
                elif first_tiles and ("tanh", first_tiles[0][0]) in done:
                    multiply_v(*first_tiles.pop(0))


        def run_scalar(n):
            while n > 0 and items:
                kind, row = items[0]
                if kind == "sigmoid" and row not in made:
                    return
                items.pop(0)
                n -= 1
                if kind == "log":
                    first, count = names_of(row)
                    m = m_bb[:, first : first + count, :]
                    nc.scalar.activation(out=m, in_=m, func=ACT.Ln, bias=ln_floor[:])
                elif kind == "sigmoid":
                    m, v = row["m"], row["v"]
                    for cols in halves if row in split else [slice(0, DB)]:
                        nc.scalar.activation(out=m[:, cols], in_=v[:, cols], func=ACT.Sigmoid, scale=-1.0)
                    if row is rf_row and not SQ_V:
                        nc.scalar.activation(out=m, in_=m, func=ACT.Square)
                else:
                    m = row["m"]
                    for cols in last_pieces if row is last_row else [slice(0, DB)]:
                        nc.scalar.activation(out=m[:, cols], in_=m[:, cols], func=ACT.Tanh, scale=-1.0)
                done.append((kind, row))

        warm_up = sums.tile([P, N_HALF], F32, tag="acc")
        for _ in range(WARM_UPS):
            nc.tensor.matmul(out=warm_up[:], lhsT=zeros[:, 0:P], rhs=zeros[:], start=True, stop=True)
        flipped_of = {0: transpose(rows[0]), 1: transpose(rows[1])}
        grouped_of = {0: regroup(flipped_of[0])}
        accs_of = {}

        def spread_bias():
            for j in range(HALVES):
                cols = slice(j * N_HALF, (j + 1) * N_HALF)
                spread = sums.tile([P, N_HALF], F32, tag="acc")
                nc.tensor.matmul(out=spread[:], lhsT=ones[:], rhs=bias_rows[:, cols], start=True, stop=True)
                nc.scalar.copy(out=bias[:, cols], in_=spread[:])

        spread_bias()
        def finish_row(i, h):
            add_bias(rows[i], accs_of[i], h)
            if h == HALVES - 1:
                made.append(rows[i])

        for i in range(len(rows) + 1):
            filling = FILL if i >= FILL_FROM else 0
            steps = [(i - 1, h) for h in range(HALVES)] if i >= 1 else []
            if i in ADD_FIRST:
                for step in steps[:ADD_N]:
                    finish_row(*step)
                steps = steps[ADD_N:]
                if not steps:
                    run_scalar(1)
            if i < len(rows):
                accs_of[i] = multiply(rows[i], quantise(grouped_of[i]))
            if i + 2 < len(rows):
                flipped_of[i + 2] = transpose(rows[i + 2])
            fill(filling)
            if len(steps) == HALVES:
                finish_row(*steps.pop(0))
                fill(filling)
            if i + 1 < len(rows) and i + 1 not in S_ROWS:
                grouped_of[i + 1] = regroup(flipped_of[i + 1])
                fill(filling)
            if steps:
                finish_row(*steps.pop(0))
                fill(filling)
            if i >= 1:
                run_scalar(S_PER if i - 1 >= len(batches[0]) else 1)
            if i + 2 in S_ROWS:
                grouped_of[i + 2] = regroup(flipped_of[i + 2], True)
        run_scalar(len(items))

        fill(len(rf_work) + len(first_tiles))
        whole = [slice(0, DB)]
        lacking_rf = list(batches[0])
        for row in [r for batch in batches[1:] for r in batch]:
            if row is last_row:
                while lacking_rf:
                    add_rf(lacking_rf.pop(0), whole)
                for i, cols in enumerate(last_pieces):
                    multiply_v(row, cols)
                    if i >= 1:
                        add_rf(row, last_pieces[i - 1 : i])
                add_rf(row, last_pieces[-1:])
            else:
                while len(lacking_rf) > 1:
                    add_rf(lacking_rf.pop(0), whole)
                multiply_v(row, whole[0])
                lacking_rf.append(row)
